import numpy as np
import ml_dtypes


def mxq(x, axis, fmt="e4m3"):
    dtype, down = {"e4m3": (ml_dtypes.float8_e4m3fn, 7), "e5m2": (ml_dtypes.float8_e5m2, 14)}[fmt]
    v = np.moveaxis(np.asarray(x, np.float32).astype(ml_dtypes.bfloat16).astype(np.float64), axis, -1)
    blocks = v.reshape(v.shape[:-1] + (-1, 32))
    amax = np.abs(blocks).max(-1, keepdims=True)
    byte = np.maximum(np.where(amax > 0, np.frexp(amax)[1] - 1 + 127, 0) - down, 1)
    scale = np.exp2(byte - 127.0)
    codes = (blocks / scale).astype(np.float32).astype(dtype).astype(np.float64)
    return np.moveaxis((codes * scale).reshape(v.shape), -1, axis)


WIDE = False


def mx_kscale(k):
    if not WIDE:
        return np.ones(k)
    levels = np.array([10, -10, 5, -5, 0])
    a = np.random.permutation(np.resize(levels, k // 512 * 4)).reshape(k // 512, 4)
    idx = np.arange(k)
    return np.exp2(a[idx // 512, idx % 128 // 32])


BF16 = ml_dtypes.bfloat16


def bf(x):
    return np.asarray(x, np.float32).astype(BF16)


def f64(x):
    return np.asarray(x).astype(np.float64)


BATCH, IN_DIM, OUT_DIM = 4096, 512, 1024


def setup_inputs():
    s = mx_kscale(IN_DIM)
    a = np.round(np.log2(s))
    x = np.random.standard_normal((BATCH, IN_DIM)) * (8.0 / np.sqrt(IN_DIM)) * s
    shift = np.round(np.random.uniform(-10.0, -1.0, (IN_DIM, OUT_DIM))) - a[:, None]
    sign = np.round(np.random.uniform(0.0, 1.0, (IN_DIM, OUT_DIM)))
    bias = np.random.standard_normal((1, OUT_DIM)) * 0.5
    return {"x": bf(x), "shift": bf(shift), "sign": bf(sign), "bias": bf(bias)}


def reference(x, shift, sign, bias):
    W = np.exp2(f64(shift)) * np.power(-1.0, f64(sign))
    return (mxq(f64(x), 1, "e4m3") @ mxq(W, 0, "e4m3")) + f64(bias)

@@ -1,0 +1,174 @@
+from contextlib import ExitStack
+
+import concourse.mybir as mybir
+from concourse.masks import make_identity
+
+F32 = mybir.dt.float32
+BF16 = mybir.dt.bfloat16
+U32 = mybir.dt.uint32
+U8 = mybir.dt.uint8
+FP8X4 = mybir.dt.float8_e4m3fn_x4
+ALU = mybir.AluOpType
+ACT = mybir.ActivationFunctionType
+
+P = 128
+BATCH, K, OUT = 4096, 512, 1024
+PACK = 4
+TILES = BATCH // P
+GROUP = 4
+GROUPS = TILES // GROUP
+HALF = 512
+WORDS = K // 2
+FLOPS = 2 * BATCH * K * OUT
+LN2 = 0.6931471805599453
+
+X_CHUNKS = ((0, 4), (4, 8), (8, 16), (16, 24), (24, 32))
+SCALAR_SHARE = ((),) * GROUPS
+STORE_CUTS = (((0, 2), (2, 4)),) + (((0, 4),),) * (GROUPS - 2) + (((0, 2), (2, 4)),)
+QUANT_AFTER = 2
+OUT_BUFS = 5
+
+
+def tile_denseshift_t_kernel(tc, x, shift, sign, bias, out):
+    nc = tc.nc
+    with ExitStack() as ctx:
+        ctx.enter_context(tc.manual_schedule())
+        keep = ctx.enter_context(tc.tile_pool(name="keep", bufs=1))
+        stage = ctx.enter_context(tc.tile_pool(name="stage", bufs=3))
+        results = ctx.enter_context(tc.tile_pool(name="results", bufs=OUT_BUFS))
+        psum_t = ctx.enter_context(tc.psum_pool(name="psum_t", bufs=2))
+        psum_acc = ctx.enter_context(tc.psum_pool(name="psum_acc", bufs=6))
+
+        warm = keep.tile([P, 1], F32, name="warm")
+        ones = keep.tile([P, P], BF16, name="ones")
+        ident = keep.tile([P, P], F32, name="ident")
+        bias_pad = keep.tile([P, OUT], BF16, name="bias_pad")
+        bias_sb = keep.tile([P, OUT], F32, name="bias_sb")
+        x_sb = keep.tile([P, TILES * K], BF16, name="x_sb")
+        shift_sb = keep.tile([P, PACK * OUT], BF16, name="shift_sb")
+        sign_sb = keep.tile([P, PACK * OUT], BF16, name="sign_sb")
+        pow_g = keep.tile([P, OUT * PACK], BF16, name="pow_g")
+        sgn_g = keep.tile([P, OUT * PACK], BF16, name="sgn_g")
+        w_g = keep.tile([P, OUT * PACK], BF16, name="w_g", align_bytes=64)
+        w_codes = keep.tile([P, OUT], U32, name="w_codes", align_bytes=64)
+        w_scales = keep.tile([P, OUT], U8, name="w_scales", align_bytes=64)
+        x_codes = keep.tile([P, BATCH], U32, name="x_codes", align_bytes=64)
+        x_scales = keep.tile([P, BATCH], U8, name="x_scales", align_bytes=64)
+
+        nc.vector.memset(warm[:], 0.0)
+        nc.vector.memset(ones[:], 1.0)
+        nc.vector.memset(bias_pad[:], 0.0)
+        make_identity(nc, ident[:])
+
+        nc.sync.dma_start(out=bias_pad[0:1, :], in_=bias)
+        for dst, src in ((shift_sb, shift), (sign_sb, sign)):
+            nc.sync.dma_start(
+                out=dst[:].rearrange("q (u r) -> q u r", u=2),
+                in_=src.rearrange("(u q e) o -> q u (e o)", u=2, e=2),
+            )
+        x_rows = x.rearrange("(p i) k -> p (i k)", i=TILES)
+        for first, last in X_CHUNKS:
+            nc.sync.dma_start(out=x_sb[:, first * K : last * K], in_=x_rows[:, first * K : last * K])
+        x_words = x_sb[:].bitcast(F32)
+        out_rows = out.rearrange("(p i) o -> p i o", i=TILES)
+
+        nc.scalar.activation(out=warm[:], in_=warm[:], func=ACT.Exp)
+
+        for h in range(2):
+            cols = slice(h * HALF, (h + 1) * HALF)
+            spread = psum_acc.tile([P, HALF], F32, tag="acc", name="spread")
+            nc.tensor.matmul(out=spread[:], lhsT=ones[:], rhs=bias_pad[:, cols], start=True, stop=True)
+            nc.vector.tensor_copy(out=bias_sb[:, cols], in_=spread[:])
+
+        def rows_view(t, h):
+            by_row = t[:].rearrange("q (t o) -> q t o", t=PACK)[:, :, h * HALF : (h + 1) * HALF]
+            return by_row.rearrange("q t (c i) -> q c t i", i=4)
+
+        def grouped_view(t, h):
+            part = t[:, h * HALF * PACK : (h + 1) * HALF * PACK]
+            return part.rearrange("q (c i t) -> q c t i", i=4, t=PACK)
+
+        def power(h):
+            nc.scalar.activation(
+                out=grouped_view(pow_g, h), in_=rows_view(shift_sb, h), func=ACT.Exp, scale=LN2
+            )
+
+        def plus_minus(h):
+            nc.vector.tensor_scalar(
+                out=grouped_view(sgn_g, h), in0=rows_view(sign_sb, h),
+                scalar1=-2.0, scalar2=1.0, op0=ALU.mult, op1=ALU.add,
+            )
+
+        def weights(h):
+            part = slice(h * HALF * PACK, (h + 1) * HALF * PACK)
+            nc.vector.tensor_tensor(out=w_g[:, part], in0=pow_g[:, part], in1=sgn_g[:, part], op=ALU.mult)
+
+        def quantise_w(h):
+            cols = slice(h * HALF, (h + 1) * HALF)
+            nc.vector.quantize_mx(
+                out=w_codes[:, cols].bitcast(FP8X4),
+                scales=w_scales[:, cols],
+                in_=w_g[:, h * HALF * PACK : (h + 1) * HALF * PACK],
+            )
+
+        def transpose_group(g):
+            x_g = stage.tile([P, GROUP * K], BF16, tag="x_g", name="x_g", align_bytes=64)
+            x_g_words = x_g[:].bitcast(F32)
+            for b in range(2):
+                xt = psum_t.tile([P, 4, P], F32, tag="xt", name="xt")
+                for pair in range(2):
+                    i = GROUP * g + 2 * b + pair
+                    for u in range(2):
+                        start = WORDS * i + P * u
+                        nc.tensor.transpose(xt[:, 2 * pair + u, :], x_words[:, start : start + P], ident[:])
+                nc.scalar.copy(
+                    out=x_g_words[:, 2 * WORDS * b : 2 * WORDS * (b + 1)].rearrange(
+                        "q (pair r u) -> q pair r u", pair=2, u=2
+                    ),
+                    in_=xt[:].rearrange("q (pair u) r -> q pair r u", u=2),
+                )
+            return x_g
+
+        def quantise_x(g, x_g):
+            cols = slice(g * GROUP * P, (g + 1) * GROUP * P)
+            nc.vector.quantize_mx(out=x_codes[:, cols].bitcast(FP8X4), scales=x_scales[:, cols], in_=x_g[:])
+
+        power(0)
+        power(1)
+        plus_minus(0)
+        weights(0)
+        plus_minus(1)
+        quantise_w(0)
+        weights(1)
+        quantise_x(0, transpose_group(0))
+        quantise_w(1)
+
+        for g in range(GROUPS):
+            x_next = transpose_group(g + 1) if g + 1 < GROUPS else None
+            o_sb = results.tile([P, GROUP, OUT], F32, tag="o_sb", name="o_sb")
+            for j in range(2 * GROUP):
+                t, h = divmod(j, 2)
+                rows = slice((GROUP * g + t) * P, (GROUP * g + t + 1) * P)
+                cols = slice(h * HALF, (h + 1) * HALF)
+                acc = psum_acc.tile([P, HALF], F32, tag="acc", name="acc")
+                nc.tensor.matmul_mx(
+                    out=acc[:],
+                    lhsT=x_codes[:, rows].bitcast(FP8X4),
+                    lhsT_scale=x_scales[:, rows],
+                    rhs=w_codes[:, cols].bitcast(FP8X4),
+                    rhs_scale=w_scales[:, cols],
+                    start=True,
+                    stop=True,
+                )
+                if j in SCALAR_SHARE[g]:
+                    nc.scalar.copy(out=o_sb[:, t, cols], in_=acc[:])
+                    nc.gpsimd.tensor_tensor(out=o_sb[:, t, cols], in0=o_sb[:, t, cols], in1=bias_sb[:, cols], op=ALU.add)
+                else:
+                    nc.vector.tensor_tensor(out=o_sb[:, t, cols], in0=acc[:], in1=bias_sb[:, cols], op=ALU.add)
+                if j == QUANT_AFTER and x_next is not None:
+                    quantise_x(g + 1, x_next)
+                for first, last in STORE_CUTS[g]:
+                    if j == 2 * last - 1:
+                        nc.sync.dma_start(
+                            out=out_rows[:, GROUP * g + first : GROUP * g + last, :], in_=o_sb[:, first:last, :]
+                        )

@@ -23,7 +23,7 @@ FLOPS = 2 * BATCH * K * OUT
 LN2 = 0.6931471805599453
 
 X_CHUNKS = ((0, 4), (4, 8), (8, 16), (16, 24), (24, 32))
-SCALAR_SHARE = ((),) * GROUPS
+SCALAR_SHARE = ((0, 4),) * GROUPS
 STORE_CUTS = (((0, 2), (2, 4)),) + (((0, 4),),) * (GROUPS - 2) + (((0, 2), (2, 4)),)
 QUANT_AFTER = 2
 OUT_BUFS = 5

@@ -23,8 +23,8 @@ FLOPS = 2 * BATCH * K * OUT
 LN2 = 0.6931471805599453
 
 X_CHUNKS = ((0, 4), (4, 8), (8, 16), (16, 24), (24, 32))
-SCALAR_SHARE = ((0, 4),) * GROUPS
-STORE_CUTS = (((0, 2), (2, 4)),) + (((0, 4),),) * (GROUPS - 2) + (((0, 2), (2, 4)),)
+SCALAR_SHARE = ((2, 4, 6), (0, 3, 6)) + ((0, 4),) * (GROUPS - 2)
+STORE_CUTS = (((0, 1), (1, 2), (2, 3), (3, 4)), ((0, 2), (2, 4))) + (((0, 4),),) * (GROUPS - 2)
 QUANT_AFTER = 2
 OUT_BUFS = 5
 
@@ -55,17 +55,18 @@ def tile_denseshift_t_kernel(tc, x, shift, sign, bias, out):
         x_codes = keep.tile([P, BATCH], U32, name="x_codes", align_bytes=64)
         x_scales = keep.tile([P, BATCH], U8, name="x_scales", align_bytes=64)
 
-        nc.vector.memset(warm[:], 0.0)
-        nc.vector.memset(ones[:], 1.0)
         nc.vector.memset(bias_pad[:], 0.0)
+        nc.vector.memset(ones[:], 1.0)
+        nc.vector.memset(warm[:], 0.0)
         make_identity(nc, ident[:])
 
-        nc.sync.dma_start(out=bias_pad[0:1, :], in_=bias)
         for dst, src in ((shift_sb, shift), (sign_sb, sign)):
             nc.sync.dma_start(
                 out=dst[:].rearrange("q (u r) -> q u r", u=2),
                 in_=src.rearrange("(u q e) o -> q u (e o)", u=2, e=2),
             )
+            if dst is shift_sb:
+                nc.sync.dma_start(out=bias_pad[0:1, :], in_=bias)
         x_rows = x.rearrange("(p i) k -> p (i k)", i=TILES)
         for first, last in X_CHUNKS:
             nc.sync.dma_start(out=x_sb[:, first * K : last * K], in_=x_rows[:, first * K : last * K])
@@ -74,11 +75,13 @@ def tile_denseshift_t_kernel(tc, x, shift, sign, bias, out):
 
         nc.scalar.activation(out=warm[:], in_=warm[:], func=ACT.Exp)
 
+        spreads = []
         for h in range(2):
-            cols = slice(h * HALF, (h + 1) * HALF)
             spread = psum_acc.tile([P, HALF], F32, tag="acc", name="spread")
-            nc.tensor.matmul(out=spread[:], lhsT=ones[:], rhs=bias_pad[:, cols], start=True, stop=True)
-            nc.vector.tensor_copy(out=bias_sb[:, cols], in_=spread[:])
+            nc.tensor.matmul(
+                out=spread[:], lhsT=ones[:], rhs=bias_pad[:, h * HALF : (h + 1) * HALF], start=True, stop=True
+            )
+            spreads.append(spread)
 
         def rows_view(t, h):
             by_row = t[:].rearrange("q (t o) -> q t o", t=PACK)[:, :, h * HALF : (h + 1) * HALF]
@@ -140,7 +143,10 @@ def tile_denseshift_t_kernel(tc, x, shift, sign, bias, out):
         plus_minus(1)
         quantise_w(0)
         weights(1)
-        quantise_x(0, transpose_group(0))
+        x_first = transpose_group(0)
+        for h in range(2):
+            nc.scalar.copy(out=bias_sb[:, h * HALF : (h + 1) * HALF], in_=spreads[h][:])
+        quantise_x(0, x_first)
         quantise_w(1)
 
         for g in range(GROUPS):

@@ -23,9 +23,8 @@ FLOPS = 2 * BATCH * K * OUT
 LN2 = 0.6931471805599453
 
 X_CHUNKS = ((0, 4), (4, 8), (8, 16), (16, 24), (24, 32))
-SCALAR_SHARE = ((2, 4, 6), (0, 3, 6)) + ((0, 4),) * (GROUPS - 2)
-STORE_CUTS = (((0, 1), (1, 2), (2, 3), (3, 4)), ((0, 2), (2, 4))) + (((0, 4),),) * (GROUPS - 2)
-QUANT_AFTER = 2
+SCALAR_BANKS = ((2, 0), (3, 0))
+HALF_STORES = (1, 2, 3)
 OUT_BUFS = 5
 
 
@@ -114,9 +113,8 @@ def tile_denseshift_t_kernel(tc, x, shift, sign, bias, out):
                 in_=w_g[:, h * HALF * PACK : (h + 1) * HALF * PACK],
             )
 
-        def transpose_group(g):
-            x_g = stage.tile([P, GROUP * K], BF16, tag="x_g", name="x_g", align_bytes=64)
-            x_g_words = x_g[:].bitcast(F32)
+        def transposes(g):
+            banks = []
             for b in range(2):
                 xt = psum_t.tile([P, 4, P], F32, tag="xt", name="xt")
                 for pair in range(2):
@@ -124,11 +122,18 @@ def tile_denseshift_t_kernel(tc, x, shift, sign, bias, out):
                     for u in range(2):
                         start = WORDS * i + P * u
                         nc.tensor.transpose(xt[:, 2 * pair + u, :], x_words[:, start : start + P], ident[:])
+                banks.append(xt)
+            return banks
+
+        def regroup(banks):
+            x_g = stage.tile([P, GROUP * K], BF16, tag="x_g", name="x_g", align_bytes=64)
+            x_g_words = x_g[:].bitcast(F32)
+            for b in range(2):
                 nc.scalar.copy(
                     out=x_g_words[:, 2 * WORDS * b : 2 * WORDS * (b + 1)].rearrange(
                         "q (pair r u) -> q pair r u", pair=2, u=2
                     ),
-                    in_=xt[:].rearrange("q (pair u) r -> q pair r u", u=2),
+                    in_=banks[b][:].rearrange("q (pair u) r -> q pair r u", u=2),
                 )
             return x_g
 
@@ -136,45 +141,75 @@ def tile_denseshift_t_kernel(tc, x, shift, sign, bias, out):
             cols = slice(g * GROUP * P, (g + 1) * GROUP * P)
             nc.vector.quantize_mx(out=x_codes[:, cols].bitcast(FP8X4), scales=x_scales[:, cols], in_=x_g[:])
 
+        def bank(g, o_sb, t, h):
+            rows = slice((GROUP * g + t) * P, (GROUP * g + t + 1) * P)
+            cols = slice(h * HALF, (h + 1) * HALF)
+            acc = psum_acc.tile([P, HALF], F32, tag="acc", name="acc")
+            nc.tensor.matmul_mx(
+                out=acc[:],
+                lhsT=x_codes[:, rows].bitcast(FP8X4),
+                lhsT_scale=x_scales[:, rows],
+                rhs=w_codes[:, cols].bitcast(FP8X4),
+                rhs_scale=w_scales[:, cols],
+                start=True,
+                stop=True,
+            )
+            if (t, h) in SCALAR_BANKS:
+                nc.scalar.copy(out=o_sb[:, t, cols], in_=acc[:])
+                nc.gpsimd.tensor_tensor(out=o_sb[:, t, cols], in0=o_sb[:, t, cols], in1=bias_sb[:, cols], op=ALU.add)
+            else:
+                nc.vector.tensor_tensor(out=o_sb[:, t, cols], in0=acc[:], in1=bias_sb[:, cols], op=ALU.add)
+
+        def store(g, o_sb, first, last):
+            nc.sync.dma_start(out=out_rows[:, GROUP * g + first : GROUP * g + last, :], in_=o_sb[:, first:last, :])
+
         power(0)
         power(1)
         plus_minus(0)
         weights(0)
         plus_minus(1)
         quantise_w(0)
-        weights(1)
-        x_first = transpose_group(0)
+        x_g = regroup(transposes(0))
         for h in range(2):
             nc.scalar.copy(out=bias_sb[:, h * HALF : (h + 1) * HALF], in_=spreads[h][:])
-        quantise_x(0, x_first)
-        quantise_w(1)
+        quantise_x(0, x_g)
+        weights(1)
 
-        for g in range(GROUPS):
-            x_next = transpose_group(g + 1) if g + 1 < GROUPS else None
+        o_sb = results.tile([P, GROUP, OUT], F32, tag="o_sb", name="o_sb")
+        banks = transposes(1)
+        for t, h in SCALAR_BANKS:
+            bank(0, o_sb, t, h)
+        x_g = regroup(banks)
+        bank(0, o_sb, 0, 0)
+        quantise_w(1)
+        bank(0, o_sb, 1, 0)
+        bank(0, o_sb, 0, 1)
+        store(0, o_sb, 0, 1)
+        bank(0, o_sb, 1, 1)
+        store(0, o_sb, 1, 2)
+        quantise_x(1, x_g)
+        bank(0, o_sb, 2, 1)
+        store(0, o_sb, 2, 3)
+        bank(0, o_sb, 3, 1)
+        store(0, o_sb, 3, 4)
+
+        for g in range(1, GROUPS):
             o_sb = results.tile([P, GROUP, OUT], F32, tag="o_sb", name="o_sb")
-            for j in range(2 * GROUP):
-                t, h = divmod(j, 2)
-                rows = slice((GROUP * g + t) * P, (GROUP * g + t + 1) * P)
-                cols = slice(h * HALF, (h + 1) * HALF)
-                acc = psum_acc.tile([P, HALF], F32, tag="acc", name="acc")
-                nc.tensor.matmul_mx(
-                    out=acc[:],
-                    lhsT=x_codes[:, rows].bitcast(FP8X4),
-                    lhsT_scale=x_scales[:, rows],
-                    rhs=w_codes[:, cols].bitcast(FP8X4),
-                    rhs_scale=w_scales[:, cols],
-                    start=True,
-                    stop=True,
-                )
-                if j in SCALAR_SHARE[g]:
-                    nc.scalar.copy(out=o_sb[:, t, cols], in_=acc[:])
-                    nc.gpsimd.tensor_tensor(out=o_sb[:, t, cols], in0=o_sb[:, t, cols], in1=bias_sb[:, cols], op=ALU.add)
-                else:
-                    nc.vector.tensor_tensor(out=o_sb[:, t, cols], in0=acc[:], in1=bias_sb[:, cols], op=ALU.add)
-                if j == QUANT_AFTER and x_next is not None:
-                    quantise_x(g + 1, x_next)
-                for first, last in STORE_CUTS[g]:
-                    if j == 2 * last - 1:
-                        nc.sync.dma_start(
-                            out=out_rows[:, GROUP * g + first : GROUP * g + last, :], in_=o_sb[:, first:last, :]
-                        )
+            if g + 1 < GROUPS:
+                x_g = regroup(transposes(g + 1))
+            for t, h in SCALAR_BANKS:
+                bank(g, o_sb, t, h)
+            bank(g, o_sb, 0, 0)
+            bank(g, o_sb, 0, 1)
+            bank(g, o_sb, 1, 0)
+            bank(g, o_sb, 1, 1)
+            if g in HALF_STORES:
+                store(g, o_sb, 0, 2)
+            if g + 1 < GROUPS:
+                quantise_x(g + 1, x_g)
+            bank(g, o_sb, 2, 1)
+            bank(g, o_sb, 3, 1)
+            if g in HALF_STORES:
+                store(g, o_sb, 2, 4)
+            else:
+                store(g, o_sb, 0, 4)

@@ -23,8 +23,9 @@ FLOPS = 2 * BATCH * K * OUT
 LN2 = 0.6931471805599453
 
 X_CHUNKS = ((0, 4), (4, 8), (8, 16), (16, 24), (24, 32))
-SCALAR_BANKS = ((2, 0), (3, 0))
-HALF_STORES = (1, 2, 3)
+SCALAR_SHARE = ((2, 4, 6), (0, 3, 6)) + ((0, 4),) * (GROUPS - 2)
+STORE_CUTS = (((0, 1), (1, 2), (2, 3), (3, 4)),) + (((0, 2), (2, 4)),) * (GROUPS - 1)
+QUANT_AFTER = 2
 OUT_BUFS = 5
 
 
@@ -113,8 +114,9 @@ def tile_denseshift_t_kernel(tc, x, shift, sign, bias, out):
                 in_=w_g[:, h * HALF * PACK : (h + 1) * HALF * PACK],
             )
 
-        def transposes(g):
-            banks = []
+        def transpose_group(g):
+            x_g = stage.tile([P, GROUP * K], BF16, tag="x_g", name="x_g", align_bytes=64)
+            x_g_words = x_g[:].bitcast(F32)
             for b in range(2):
                 xt = psum_t.tile([P, 4, P], F32, tag="xt", name="xt")
                 for pair in range(2):
@@ -122,18 +124,11 @@ def tile_denseshift_t_kernel(tc, x, shift, sign, bias, out):
                     for u in range(2):
                         start = WORDS * i + P * u
                         nc.tensor.transpose(xt[:, 2 * pair + u, :], x_words[:, start : start + P], ident[:])
-                banks.append(xt)
-            return banks
-
-        def regroup(banks):
-            x_g = stage.tile([P, GROUP * K], BF16, tag="x_g", name="x_g", align_bytes=64)
-            x_g_words = x_g[:].bitcast(F32)
-            for b in range(2):
                 nc.scalar.copy(
                     out=x_g_words[:, 2 * WORDS * b : 2 * WORDS * (b + 1)].rearrange(
                         "q (pair r u) -> q pair r u", pair=2, u=2
                     ),
-                    in_=banks[b][:].rearrange("q (pair u) r -> q pair r u", u=2),
+                    in_=xt[:].rearrange("q (pair u) r -> q pair r u", u=2),
                 )
             return x_g
 
@@ -141,75 +136,45 @@ def tile_denseshift_t_kernel(tc, x, shift, sign, bias, out):
             cols = slice(g * GROUP * P, (g + 1) * GROUP * P)
             nc.vector.quantize_mx(out=x_codes[:, cols].bitcast(FP8X4), scales=x_scales[:, cols], in_=x_g[:])
 
-        def bank(g, o_sb, t, h):
-            rows = slice((GROUP * g + t) * P, (GROUP * g + t + 1) * P)
-            cols = slice(h * HALF, (h + 1) * HALF)
-            acc = psum_acc.tile([P, HALF], F32, tag="acc", name="acc")
-            nc.tensor.matmul_mx(
-                out=acc[:],
-                lhsT=x_codes[:, rows].bitcast(FP8X4),
-                lhsT_scale=x_scales[:, rows],
-                rhs=w_codes[:, cols].bitcast(FP8X4),
-                rhs_scale=w_scales[:, cols],
-                start=True,
-                stop=True,
-            )
-            if (t, h) in SCALAR_BANKS:
-                nc.scalar.copy(out=o_sb[:, t, cols], in_=acc[:])
-                nc.gpsimd.tensor_tensor(out=o_sb[:, t, cols], in0=o_sb[:, t, cols], in1=bias_sb[:, cols], op=ALU.add)
-            else:
-                nc.vector.tensor_tensor(out=o_sb[:, t, cols], in0=acc[:], in1=bias_sb[:, cols], op=ALU.add)
-
-        def store(g, o_sb, first, last):
-            nc.sync.dma_start(out=out_rows[:, GROUP * g + first : GROUP * g + last, :], in_=o_sb[:, first:last, :])
-
         power(0)
         power(1)
         plus_minus(0)
         weights(0)
         plus_minus(1)
         quantise_w(0)
-        x_g = regroup(transposes(0))
+        weights(1)
+        x_first = transpose_group(0)
         for h in range(2):
             nc.scalar.copy(out=bias_sb[:, h * HALF : (h + 1) * HALF], in_=spreads[h][:])
-        quantise_x(0, x_g)
-        weights(1)
-
-        o_sb = results.tile([P, GROUP, OUT], F32, tag="o_sb", name="o_sb")
-        banks = transposes(1)
-        for t, h in SCALAR_BANKS:
-            bank(0, o_sb, t, h)
-        x_g = regroup(banks)
-        bank(0, o_sb, 0, 0)
+        quantise_x(0, x_first)
         quantise_w(1)
-        bank(0, o_sb, 1, 0)
-        bank(0, o_sb, 0, 1)
-        store(0, o_sb, 0, 1)
-        bank(0, o_sb, 1, 1)
-        store(0, o_sb, 1, 2)
-        quantise_x(1, x_g)
-        bank(0, o_sb, 2, 1)
-        store(0, o_sb, 2, 3)
-        bank(0, o_sb, 3, 1)
-        store(0, o_sb, 3, 4)
 
-        for g in range(1, GROUPS):
+        for g in range(GROUPS):
+            x_next = transpose_group(g + 1) if g + 1 < GROUPS else None
             o_sb = results.tile([P, GROUP, OUT], F32, tag="o_sb", name="o_sb")
-            if g + 1 < GROUPS:
-                x_g = regroup(transposes(g + 1))
-            for t, h in SCALAR_BANKS:
-                bank(g, o_sb, t, h)
-            bank(g, o_sb, 0, 0)
-            bank(g, o_sb, 0, 1)
-            bank(g, o_sb, 1, 0)
-            bank(g, o_sb, 1, 1)
-            if g in HALF_STORES:
-                store(g, o_sb, 0, 2)
-            if g + 1 < GROUPS:
-                quantise_x(g + 1, x_g)
-            bank(g, o_sb, 2, 1)
-            bank(g, o_sb, 3, 1)
-            if g in HALF_STORES:
-                store(g, o_sb, 2, 4)
-            else:
-                store(g, o_sb, 0, 4)
+            for j in range(2 * GROUP):
+                t, h = divmod(j, 2)
+                rows = slice((GROUP * g + t) * P, (GROUP * g + t + 1) * P)
+                cols = slice(h * HALF, (h + 1) * HALF)
+                acc = psum_acc.tile([P, HALF], F32, tag="acc", name="acc")
+                nc.tensor.matmul_mx(
+                    out=acc[:],
+                    lhsT=x_codes[:, rows].bitcast(FP8X4),
+                    lhsT_scale=x_scales[:, rows],
+                    rhs=w_codes[:, cols].bitcast(FP8X4),
+                    rhs_scale=w_scales[:, cols],
+                    start=True,
+                    stop=True,
+                )
+                if j in SCALAR_SHARE[g]:
+                    nc.scalar.copy(out=o_sb[:, t, cols], in_=acc[:])
+                    nc.gpsimd.tensor_tensor(out=o_sb[:, t, cols], in0=o_sb[:, t, cols], in1=bias_sb[:, cols], op=ALU.add)
+                else:
+                    nc.vector.tensor_tensor(out=o_sb[:, t, cols], in0=acc[:], in1=bias_sb[:, cols], op=ALU.add)
+                if j == QUANT_AFTER and x_next is not None:
+                    quantise_x(g + 1, x_next)
+                for first, last in STORE_CUTS[g]:
+                    if j == 2 * last - 1:
+                        nc.sync.dma_start(
+                            out=out_rows[:, GROUP * g + first : GROUP * g + last, :], in_=o_sb[:, first:last, :]
+                        )

@@ -23,9 +23,9 @@ FLOPS = 2 * BATCH * K * OUT
 LN2 = 0.6931471805599453
 
 X_CHUNKS = ((0, 4), (4, 8), (8, 16), (16, 24), (24, 32))
-SCALAR_SHARE = ((2, 4, 6), (0, 3, 6)) + ((0, 4),) * (GROUPS - 2)
-STORE_CUTS = (((0, 1), (1, 2), (2, 3), (3, 4)),) + (((0, 2), (2, 4)),) * (GROUPS - 1)
-QUANT_AFTER = 2
+SCALAR_SHARE = ((2, 6),) * GROUPS
+STORE_CUTS = (((0, 1), (1, 2), (2, 3), (3, 4)), ((0, 2), (2, 4))) + (((0, 4),),) * (GROUPS - 2)
+QUANT_AFTER = 0
 OUT_BUFS = 5
 
 

from contextlib import ExitStack

import concourse.mybir as mybir
from concourse.masks import make_identity

F32 = mybir.dt.float32
BF16 = mybir.dt.bfloat16
U32 = mybir.dt.uint32
U8 = mybir.dt.uint8
FP8X4 = mybir.dt.float8_e4m3fn_x4
ALU = mybir.AluOpType
ACT = mybir.ActivationFunctionType

P = 128
BATCH, K, OUT = 4096, 512, 1024
PACK = 4
TILES = BATCH // P
GROUP = 4
GROUPS = TILES // GROUP
HALF = 512
WORDS = K // 2
FLOPS = 2 * BATCH * K * OUT
LN2 = 0.6931471805599453

X_CHUNKS = ((0, 4), (4, 8), (8, 16), (16, 24), (24, 32))
SCALAR_SHARE = ((2, 6),) * GROUPS
STORE_CUTS = (((0, 1), (1, 2), (2, 3), (3, 4)), ((0, 2), (2, 4))) + (((0, 4),),) * (GROUPS - 2)
QUANT_AFTER = 0
OUT_BUFS = 5


def tile_denseshift_t_kernel(tc, x, shift, sign, bias, out):
    nc = tc.nc
    with ExitStack() as ctx:
        ctx.enter_context(tc.manual_schedule())
        keep = ctx.enter_context(tc.tile_pool(name="keep", bufs=1))
        stage = ctx.enter_context(tc.tile_pool(name="stage", bufs=3))
        results = ctx.enter_context(tc.tile_pool(name="results", bufs=OUT_BUFS))
        psum_t = ctx.enter_context(tc.psum_pool(name="psum_t", bufs=2))
        psum_acc = ctx.enter_context(tc.psum_pool(name="psum_acc", bufs=6))

        warm = keep.tile([P, 1], F32, name="warm")
        ones = keep.tile([P, P], BF16, name="ones")
        ident = keep.tile([P, P], F32, name="ident")
        bias_pad = keep.tile([P, OUT], BF16, name="bias_pad")
        bias_sb = keep.tile([P, OUT], F32, name="bias_sb")
        x_sb = keep.tile([P, TILES * K], BF16, name="x_sb")
        shift_sb = keep.tile([P, PACK * OUT], BF16, name="shift_sb")
        sign_sb = keep.tile([P, PACK * OUT], BF16, name="sign_sb")
        pow_g = keep.tile([P, OUT * PACK], BF16, name="pow_g")
        sgn_g = keep.tile([P, OUT * PACK], BF16, name="sgn_g")
        w_g = keep.tile([P, OUT * PACK], BF16, name="w_g", align_bytes=64)
        w_codes = keep.tile([P, OUT], U32, name="w_codes", align_bytes=64)
        w_scales = keep.tile([P, OUT], U8, name="w_scales", align_bytes=64)
        x_codes = keep.tile([P, BATCH], U32, name="x_codes", align_bytes=64)
        x_scales = keep.tile([P, BATCH], U8, name="x_scales", align_bytes=64)

        nc.vector.memset(bias_pad[:], 0.0)
        nc.vector.memset(ones[:], 1.0)
        nc.vector.memset(warm[:], 0.0)
        make_identity(nc, ident[:])

        for dst, src in ((shift_sb, shift), (sign_sb, sign)):
            nc.sync.dma_start(
                out=dst[:].rearrange("q (u r) -> q u r", u=2),
                in_=src.rearrange("(u q e) o -> q u (e o)", u=2, e=2),
            )
            if dst is shift_sb:
                nc.sync.dma_start(out=bias_pad[0:1, :], in_=bias)
        x_rows = x.rearrange("(p i) k -> p (i k)", i=TILES)
        for first, last in X_CHUNKS:
            nc.sync.dma_start(out=x_sb[:, first * K : last * K], in_=x_rows[:, first * K : last * K])
        x_words = x_sb[:].bitcast(F32)
        out_rows = out.rearrange("(p i) o -> p i o", i=TILES)

        nc.scalar.activation(out=warm[:], in_=warm[:], func=ACT.Exp)

        spreads = []
        for h in range(2):
            spread = psum_acc.tile([P, HALF], F32, tag="acc", name="spread")
            nc.tensor.matmul(
                out=spread[:], lhsT=ones[:], rhs=bias_pad[:, h * HALF : (h + 1) * HALF], start=True, stop=True
            )
            spreads.append(spread)

        def rows_view(t, h):
            by_row = t[:].rearrange("q (t o) -> q t o", t=PACK)[:, :, h * HALF : (h + 1) * HALF]
            return by_row.rearrange("q t (c i) -> q c t i", i=4)

        def grouped_view(t, h):
            part = t[:, h * HALF * PACK : (h + 1) * HALF * PACK]
            return part.rearrange("q (c i t) -> q c t i", i=4, t=PACK)

        def power(h):
            nc.scalar.activation(
                out=grouped_view(pow_g, h), in_=rows_view(shift_sb, h), func=ACT.Exp, scale=LN2
            )

        def plus_minus(h):
            nc.vector.tensor_scalar(
                out=grouped_view(sgn_g, h), in0=rows_view(sign_sb, h),
                scalar1=-2.0, scalar2=1.0, op0=ALU.mult, op1=ALU.add,
            )

        def weights(h):
            part = slice(h * HALF * PACK, (h + 1) * HALF * PACK)
            nc.vector.tensor_tensor(out=w_g[:, part], in0=pow_g[:, part], in1=sgn_g[:, part], op=ALU.mult)

        def quantise_w(h):
            cols = slice(h * HALF, (h + 1) * HALF)
            nc.vector.quantize_mx(
                out=w_codes[:, cols].bitcast(FP8X4),
                scales=w_scales[:, cols],
                in_=w_g[:, h * HALF * PACK : (h + 1) * HALF * PACK],
            )

        def transpose_group(g):
            x_g = stage.tile([P, GROUP * K], BF16, tag="x_g", name="x_g", align_bytes=64)
            x_g_words = x_g[:].bitcast(F32)
            for b in range(2):
                xt = psum_t.tile([P, 4, P], F32, tag="xt", name="xt")
                for pair in range(2):
                    i = GROUP * g + 2 * b + pair
                    for u in range(2):
                        start = WORDS * i + P * u
                        nc.tensor.transpose(xt[:, 2 * pair + u, :], x_words[:, start : start + P], ident[:])
                nc.scalar.copy(
                    out=x_g_words[:, 2 * WORDS * b : 2 * WORDS * (b + 1)].rearrange(
                        "q (pair r u) -> q pair r u", pair=2, u=2
                    ),
                    in_=xt[:].rearrange("q (pair u) r -> q pair r u", u=2),
                )
            return x_g

        def quantise_x(g, x_g):
            cols = slice(g * GROUP * P, (g + 1) * GROUP * P)
            nc.vector.quantize_mx(out=x_codes[:, cols].bitcast(FP8X4), scales=x_scales[:, cols], in_=x_g[:])

        power(0)
        power(1)
        plus_minus(0)
        weights(0)
        plus_minus(1)
        quantise_w(0)
        weights(1)
        x_first = transpose_group(0)
        for h in range(2):
            nc.scalar.copy(out=bias_sb[:, h * HALF : (h + 1) * HALF], in_=spreads[h][:])
        quantise_x(0, x_first)
        quantise_w(1)

        for g in range(GROUPS):
            x_next = transpose_group(g + 1) if g + 1 < GROUPS else None
            o_sb = results.tile([P, GROUP, OUT], F32, tag="o_sb", name="o_sb")
            for j in range(2 * GROUP):
                t, h = divmod(j, 2)
                rows = slice((GROUP * g + t) * P, (GROUP * g + t + 1) * P)
                cols = slice(h * HALF, (h + 1) * HALF)
                acc = psum_acc.tile([P, HALF], F32, tag="acc", name="acc")
                nc.tensor.matmul_mx(
                    out=acc[:],
                    lhsT=x_codes[:, rows].bitcast(FP8X4),
                    lhsT_scale=x_scales[:, rows],
                    rhs=w_codes[:, cols].bitcast(FP8X4),
                    rhs_scale=w_scales[:, cols],
                    start=True,
                    stop=True,
                )
                if j in SCALAR_SHARE[g]:
                    nc.scalar.copy(out=o_sb[:, t, cols], in_=acc[:])
                    nc.gpsimd.tensor_tensor(out=o_sb[:, t, cols], in0=o_sb[:, t, cols], in1=bias_sb[:, cols], op=ALU.add)
                else:
                    nc.vector.tensor_tensor(out=o_sb[:, t, cols], in0=acc[:], in1=bias_sb[:, cols], op=ALU.add)
                if j == QUANT_AFTER and x_next is not None:
                    quantise_x(g + 1, x_next)
                for first, last in STORE_CUTS[g]:
                    if j == 2 * last - 1:
                        nc.sync.dma_start(
                            out=out_rows[:, GROUP * g + first : GROUP * g + last, :], in_=o_sb[:, first:last, :]
                        )
